import numpy as np
import ml_dtypes

BF16 = ml_dtypes.bfloat16


def bf(x):
    return np.asarray(x, np.float32).astype(BF16)


def f32(x):
    return np.asarray(x, np.float32)


def f64(x):
    return np.asarray(x).astype(np.float64)


def striped(idx):
    return np.tile(idx.reshape(-1, 16).T, (8, 1))


C, S, K, N, H = 256, 256, 4, 1024, 128


def setup_inputs():
    idx = np.concatenate([np.random.permutation(S)[:H] for _ in range(N // H)])
    return {"x": f32(np.random.standard_normal((C, S))), "perm": f32(np.tile(np.random.standard_normal((1, K * N)), (C, 1))), "offs": striped(idx)}


def reference(x, perm, offs):
    idx = offs[:16].T.reshape(-1)
    picked = f64(x)[:, idx]
    prod = picked[:, None, :] * f64(perm).reshape(C, K, N)
    return prod.reshape(C, K, K, S).sum(axis=2).reshape(C, K * S)

@@ -1,0 +1,58 @@
+import concourse.mybir as mybir
+
+F32 = mybir.dt.float32
+U16 = mybir.dt.uint16
+MULT = mybir.AluOpType.mult
+ADD = mybir.AluOpType.add
+
+P = 128
+C = 256
+S = 256
+K = 4
+M = 4
+N = K * S
+PER_COLUMN = 16
+
+
+def tile_paiconvmax_kernel(tc, x, perm, offs, out):
+    nc = tc.nc
+    blocks = C // P
+    with (
+        tc.tile_pool(name="held", bufs=1) as held,
+        tc.tile_pool(name="work", bufs=3) as work,
+    ):
+        offsets = held.tile([P, N // PER_COLUMN], U16, name="offsets")
+        nc.sync.dma_start(offsets[:], offs)
+
+        windows = []
+        weights = []
+        for b in range(blocks):
+            rows = slice(b * P, (b + 1) * P)
+            window = held.tile([P, S], F32, name=f"window{b}")
+            nc.scalar.dma_start(window[:], x[rows, :])
+            windows.append(window)
+            for m in range(M):
+                weight = held.tile([P, N], F32, name=f"weight{b}_{m}")
+                queue = nc.sync if m % 2 == 0 else nc.scalar
+                queue.dma_start(weight[:], perm[rows, m * N : (m + 1) * N])
+                weights.append(weight)
+
+        for b in range(blocks):
+            rows = slice(b * P, (b + 1) * P)
+            for m in range(M):
+                weight = weights[b * M + m]
+                product = work.tile([P, N], F32, name="product")
+                for k in range(K):
+                    piece = slice(k * S, (k + 1) * S)
+                    columns = slice(k * S // PER_COLUMN, (k + 1) * S // PER_COLUMN)
+                    nc.vector.tensor_tensor(
+                        product[:, piece],
+                        windows[b][:].indirect(offsets[:, columns]),
+                        weight[:, piece],
+                        MULT,
+                    )
+                pairs = work.tile([P, 2 * S], F32, name="pairs")
+                nc.vector.tensor_tensor(pairs[:], product[:, : 2 * S], product[:, 2 * S :], ADD)
+                mixed = work.tile([P, S], F32, name="mixed")
+                nc.vector.tensor_tensor(mixed[:], pairs[:, :S], pairs[:, S:], ADD)
+                nc.sync.dma_start(out[rows, m * S : (m + 1) * S], mixed[:])

@@ -1,9 +1,9 @@
 import concourse.mybir as mybir
+from concourse.masks import make_identity
 
 F32 = mybir.dt.float32
 U16 = mybir.dt.uint16
 MULT = mybir.AluOpType.mult
-ADD = mybir.AluOpType.add
 
 P = 128
 C = 256
@@ -19,7 +19,8 @@ def tile_paiconvmax_kernel(tc, x, perm, offs, out):
     blocks = C // P
     with (
         tc.tile_pool(name="held", bufs=1) as held,
-        tc.tile_pool(name="work", bufs=3) as work,
+        tc.tile_pool(name="work", bufs=4) as work,
+        tc.psum_pool(name="psum", bufs=4) as psum,
     ):
         offsets = held.tile([P, N // PER_COLUMN], U16, name="offsets")
         nc.sync.dma_start(offsets[:], offs)
@@ -37,11 +38,15 @@ def tile_paiconvmax_kernel(tc, x, perm, offs, out):
                 queue.dma_start(weight[:], perm[rows, m * N : (m + 1) * N])
                 weights.append(weight)
 
+        identity = held.tile([P, P], F32, name="identity")
+        make_identity(nc, identity[:])
+
         for b in range(blocks):
             rows = slice(b * P, (b + 1) * P)
             for m in range(M):
                 weight = weights[b * M + m]
                 product = work.tile([P, N], F32, name="product")
+                total = psum.tile([P, S], F32, name="total")
                 for k in range(K):
                     piece = slice(k * S, (k + 1) * S)
                     columns = slice(k * S // PER_COLUMN, (k + 1) * S // PER_COLUMN)
@@ -51,8 +56,7 @@ def tile_paiconvmax_kernel(tc, x, perm, offs, out):
                         weight[:, piece],
                         MULT,
                     )
-                pairs = work.tile([P, 2 * S], F32, name="pairs")
-                nc.vector.tensor_tensor(pairs[:], product[:, : 2 * S], product[:, 2 * S :], ADD)
+                    nc.tensor.matmul(total[:], identity[:], product[:, piece], start=(k == 0), stop=(k == K - 1))
                 mixed = work.tile([P, S], F32, name="mixed")
-                nc.vector.tensor_tensor(mixed[:], pairs[:, :S], pairs[:, S:], ADD)
+                nc.scalar.copy(mixed[:], total[:])
                 nc.sync.dma_start(out[rows, m * S : (m + 1) * S], mixed[:])

@@ -30,12 +30,13 @@ def tile_paiconvmax_kernel(tc, x, perm, offs, out):
         for b in range(blocks):
             rows = slice(b * P, (b + 1) * P)
             window = held.tile([P, S], F32, name=f"window{b}")
-            nc.scalar.dma_start(window[:], x[rows, :])
+            nc.gpsimd.dma_start(window[:], x[rows, :])
             windows.append(window)
             for m in range(M):
                 weight = held.tile([P, N], F32, name=f"weight{b}_{m}")
-                queue = nc.sync if m % 2 == 0 else nc.scalar
-                queue.dma_start(weight[:], perm[rows, m * N : (m + 1) * N])
+                for k in range(K):
+                    queue = nc.scalar if k % 2 == 0 else nc.sync
+                    queue.dma_start(weight[:, k * S : (k + 1) * S], perm[rows, m * N + k * S : m * N + (k + 1) * S])
                 weights.append(weight)
 
         identity = held.tile([P, P], F32, name="identity")

@@ -30,13 +30,12 @@ def tile_paiconvmax_kernel(tc, x, perm, offs, out):
         for b in range(blocks):
             rows = slice(b * P, (b + 1) * P)
             window = held.tile([P, S], F32, name=f"window{b}")
-            nc.gpsimd.dma_start(window[:], x[rows, :])
+            nc.scalar.dma_start(window[:], x[rows, :])
             windows.append(window)
             for m in range(M):
                 weight = held.tile([P, N], F32, name=f"weight{b}_{m}")
                 for k in range(K):
-                    queue = nc.scalar if k % 2 == 0 else nc.sync
-                    queue.dma_start(weight[:, k * S : (k + 1) * S], perm[rows, m * N + k * S : m * N + (k + 1) * S])
+                    nc.sync.dma_start(weight[:, k * S : (k + 1) * S], perm[rows, m * N + k * S : m * N + (k + 1) * S])
                 weights.append(weight)
 
         identity = held.tile([P, P], F32, name="identity")
@@ -60,4 +59,4 @@ def tile_paiconvmax_kernel(tc, x, perm, offs, out):
                     nc.tensor.matmul(total[:], identity[:], product[:, piece], start=(k == 0), stop=(k == K - 1))
                 mixed = work.tile([P, S], F32, name="mixed")
                 nc.scalar.copy(mixed[:], total[:])
-                nc.sync.dma_start(out[rows, m * S : (m + 1) * S], mixed[:])
+                nc.scalar.dma_start(out[rows, m * S : (m + 1) * S], mixed[:])

@@ -4,6 +4,7 @@ from concourse.masks import make_identity
 F32 = mybir.dt.float32
 U16 = mybir.dt.uint16
 MULT = mybir.AluOpType.mult
+ADD = mybir.AluOpType.add
 
 P = 128
 C = 256
@@ -45,8 +46,11 @@ def tile_paiconvmax_kernel(tc, x, perm, offs, out):
             rows = slice(b * P, (b + 1) * P)
             for m in range(M):
                 weight = weights[b * M + m]
+                last_unit = b == blocks - 1 and m == M - 1
                 product = work.tile([P, N], F32, name="product")
                 total = psum.tile([P, S], F32, name="total")
+                mixed = work.tile([P, S], F32, name="mixed")
+                summed = K - 1 if last_unit else K
                 for k in range(K):
                     piece = slice(k * S, (k + 1) * S)
                     columns = slice(k * S // PER_COLUMN, (k + 1) * S // PER_COLUMN)
@@ -56,7 +60,10 @@ def tile_paiconvmax_kernel(tc, x, perm, offs, out):
                         weight[:, piece],
                         MULT,
                     )
-                    nc.tensor.matmul(total[:], identity[:], product[:, piece], start=(k == 0), stop=(k == K - 1))
-                mixed = work.tile([P, S], F32, name="mixed")
-                nc.scalar.copy(mixed[:], total[:])
+                    if k < summed:
+                        nc.tensor.matmul(total[:], identity[:], product[:, piece], start=(k == 0), stop=(k == summed - 1))
+                if last_unit:
+                    nc.vector.tensor_tensor(mixed[:], product[:, (K - 1) * S : K * S], total[:], ADD)
+                else:
+                    nc.scalar.copy(mixed[:], total[:])
                 nc.scalar.dma_start(out[rows, m * S : (m + 1) * S], mixed[:])

@@ -24,19 +24,21 @@ def tile_paiconvmax_kernel(tc, x, perm, offs, out):
         tc.psum_pool(name="psum", bufs=4) as psum,
     ):
         offsets = held.tile([P, N // PER_COLUMN], U16, name="offsets")
-        nc.sync.dma_start(offsets[:], offs)
 
         windows = []
         weights = []
         for b in range(blocks):
             rows = slice(b * P, (b + 1) * P)
             window = held.tile([P, S], F32, name=f"window{b}")
-            nc.scalar.dma_start(window[:], x[rows, :])
+            window_queue = nc.scalar if b == 0 else nc.sync
+            window_queue.dma_start(window[:], x[rows, :])
             windows.append(window)
             for m in range(M):
                 weight = held.tile([P, N], F32, name=f"weight{b}_{m}")
                 for k in range(K):
                     nc.sync.dma_start(weight[:, k * S : (k + 1) * S], perm[rows, m * N + k * S : m * N + (k + 1) * S])
+                    if b == 0 and m == 0 and k == 0:
+                        nc.sync.dma_start(offsets[:], offs)
                 weights.append(weight)
 
         identity = held.tile([P, P], F32, name="identity")

@@ -14,6 +14,8 @@ M = 4
 N = K * S
 PER_COLUMN = 16
 
+BYTES = C * S * 4 + M * N * 4 + P * (N // PER_COLUMN) * 2 + C * M * S * 4
+
 
 def tile_paiconvmax_kernel(tc, x, perm, offs, out):
     nc = tc.nc
@@ -25,21 +27,17 @@ def tile_paiconvmax_kernel(tc, x, perm, offs, out):
     ):
         offsets = held.tile([P, N // PER_COLUMN], U16, name="offsets")
 
-        windows = []
+        windows = [held.tile([P, S], F32, name=f"window{b}") for b in range(blocks)]
+        nc.scalar.dma_start(windows[0][:], x[0:P, :])
         weights = []
-        for b in range(blocks):
-            rows = slice(b * P, (b + 1) * P)
-            window = held.tile([P, S], F32, name=f"window{b}")
-            window_queue = nc.scalar if b == 0 else nc.sync
-            window_queue.dma_start(window[:], x[rows, :])
-            windows.append(window)
-            for m in range(M):
-                weight = held.tile([P, N], F32, name=f"weight{b}_{m}")
-                for k in range(K):
-                    nc.sync.dma_start(weight[:, k * S : (k + 1) * S], perm[rows, m * N + k * S : m * N + (k + 1) * S])
-                    if b == 0 and m == 0 and k == 0:
-                        nc.sync.dma_start(offsets[:], offs)
-                weights.append(weight)
+        for m in range(M):
+            weight = held.tile([P, N], F32, name=f"weight{m}")
+            for k in range(K):
+                nc.sync.dma_start(weight[:, k * S : (k + 1) * S], perm[0:P, m * N + k * S : m * N + (k + 1) * S])
+                if m == 0 and k == 0:
+                    nc.sync.dma_start(offsets[:], offs)
+            weights.append(weight)
+        nc.sync.dma_start(windows[1][:], x[P : 2 * P, :])
 
         identity = held.tile([P, P], F32, name="identity")
         make_identity(nc, identity[:])
@@ -47,7 +45,7 @@ def tile_paiconvmax_kernel(tc, x, perm, offs, out):
         for b in range(blocks):
             rows = slice(b * P, (b + 1) * P)
             for m in range(M):
-                weight = weights[b * M + m]
+                weight = weights[m]
                 last_unit = b == blocks - 1 and m == M - 1
                 product = work.tile([P, N], F32, name="product")
                 total = psum.tile([P, S], F32, name="total")

@@ -29,14 +29,15 @@ def tile_paiconvmax_kernel(tc, x, perm, offs, out):
 
         windows = [held.tile([P, S], F32, name=f"window{b}") for b in range(blocks)]
         nc.scalar.dma_start(windows[0][:], x[0:P, :])
-        weights = []
-        for m in range(M):
-            weight = held.tile([P, N], F32, name=f"weight{m}")
-            for k in range(K):
-                nc.sync.dma_start(weight[:, k * S : (k + 1) * S], perm[0:P, m * N + k * S : m * N + (k + 1) * S])
-                if m == 0 and k == 0:
-                    nc.sync.dma_start(offsets[:], offs)
-            weights.append(weight)
+        weights = [held.tile([P, N], F32, name=f"weight{m}") for m in range(M)]
+        asked = 0
+        while asked < M * N:
+            m, start = divmod(asked, N)
+            width = min(max(asked, S), N - start)
+            nc.sync.dma_start(weights[m][:, start : start + width], perm[0:P, asked : asked + width])
+            if asked == 0:
+                nc.sync.dma_start(offsets[:], offs)
+            asked += width
         nc.sync.dma_start(windows[1][:], x[P : 2 * P, :])
 
         identity = held.tile([P, P], F32, name="identity")

@@ -13,6 +13,7 @@ K = 4
 M = 4
 N = K * S
 PER_COLUMN = 16
+FIRST = 64
 
 BYTES = C * S * 4 + M * N * 4 + P * (N // PER_COLUMN) * 2 + C * M * S * 4
 
@@ -28,17 +29,18 @@ def tile_paiconvmax_kernel(tc, x, perm, offs, out):
         offsets = held.tile([P, N // PER_COLUMN], U16, name="offsets")
 
         windows = [held.tile([P, S], F32, name=f"window{b}") for b in range(blocks)]
-        nc.scalar.dma_start(windows[0][:], x[0:P, :])
         weights = [held.tile([P, N], F32, name=f"weight{m}") for m in range(M)]
-        asked = 0
+        nc.scalar.dma_start(windows[0][:], x[0:P, :])
+        nc.sync.dma_start(weights[0][:, :FIRST], perm[0:P, :FIRST])
+        nc.sync.dma_start(offsets[:], offs)
+        nc.scalar.dma_start(weights[0][:, FIRST:S], perm[0:P, FIRST:S])
+        asked = S
         while asked < M * N:
             m, start = divmod(asked, N)
-            width = min(max(asked, S), N - start)
-            nc.sync.dma_start(weights[m][:, start : start + width], perm[0:P, asked : asked + width])
-            if asked == 0:
-                nc.sync.dma_start(offsets[:], offs)
+            width = min(asked, N - start)
+            nc.scalar.dma_start(weights[m][:, start : start + width], perm[0:P, asked : asked + width])
             asked += width
-        nc.sync.dma_start(windows[1][:], x[P : 2 * P, :])
+        nc.scalar.dma_start(windows[1][:], x[P : 2 * P, :])
 
         identity = held.tile([P, P], F32, name="identity")
         make_identity(nc, identity[:])
@@ -47,22 +49,24 @@ def tile_paiconvmax_kernel(tc, x, perm, offs, out):
             rows = slice(b * P, (b + 1) * P)
             for m in range(M):
                 weight = weights[m]
+                first_unit = b == 0 and m == 0
                 last_unit = b == blocks - 1 and m == M - 1
                 product = work.tile([P, N], F32, name="product")
                 total = psum.tile([P, S], F32, name="total")
                 mixed = work.tile([P, S], F32, name="mixed")
                 summed = K - 1 if last_unit else K
                 for k in range(K):
-                    piece = slice(k * S, (k + 1) * S)
-                    columns = slice(k * S // PER_COLUMN, (k + 1) * S // PER_COLUMN)
-                    nc.vector.tensor_tensor(
-                        product[:, piece],
-                        windows[b][:].indirect(offsets[:, columns]),
-                        weight[:, piece],
-                        MULT,
-                    )
+                    cuts = [0, FIRST, S] if first_unit and k == 0 else [0, S]
+                    for low, high in zip(cuts[:-1], cuts[1:]):
+                        entries = slice(k * S + low, k * S + high)
+                        nc.vector.tensor_tensor(
+                            product[:, entries],
+                            windows[b][:].indirect(offsets[:, entries.start // PER_COLUMN : entries.stop // PER_COLUMN]),
+                            weight[:, entries],
+                            MULT,
+                        )
                     if k < summed:
-                        nc.tensor.matmul(total[:], identity[:], product[:, piece], start=(k == 0), stop=(k == summed - 1))
+                        nc.tensor.matmul(total[:], identity[:], product[:, k * S : (k + 1) * S], start=(k == 0), stop=(k == summed - 1))
                 if last_unit:
                     nc.vector.tensor_tensor(mixed[:], product[:, (K - 1) * S : K * S], total[:], ADD)
                 else:

@@ -37,7 +37,7 @@ def tile_paiconvmax_kernel(tc, x, perm, offs, out):
         asked = S
         while asked < M * N:
             m, start = divmod(asked, N)
-            width = min(asked, N - start)
+            width = min(max(asked // (2 * S), 1) * S, N - start)
             nc.scalar.dma_start(weights[m][:, start : start + width], perm[0:P, asked : asked + width])
             asked += width
         nc.scalar.dma_start(windows[1][:], x[P : 2 * P, :])

@@ -13,6 +13,7 @@ K = 4
 M = 4
 N = K * S
 PER_COLUMN = 16
+PIECES = 2 * K
 FIRST = 64
 
 BYTES = C * S * 4 + M * N * 4 + P * (N // PER_COLUMN) * 2 + C * M * S * 4
@@ -23,7 +24,7 @@ def tile_paiconvmax_kernel(tc, x, perm, offs, out):
     blocks = C // P
     with (
         tc.tile_pool(name="held", bufs=1) as held,
-        tc.tile_pool(name="work", bufs=4) as work,
+        tc.tile_pool(name="work", bufs=PIECES) as work,
         tc.psum_pool(name="psum", bufs=4) as psum,
     ):
         offsets = held.tile([P, N // PER_COLUMN], U16, name="offsets")
@@ -47,28 +48,38 @@ def tile_paiconvmax_kernel(tc, x, perm, offs, out):
 
         for b in range(blocks):
             rows = slice(b * P, (b + 1) * P)
-            for m in range(M):
-                weight = weights[m]
-                first_unit = b == 0 and m == 0
-                last_unit = b == blocks - 1 and m == M - 1
-                product = work.tile([P, N], F32, name="product")
-                total = psum.tile([P, S], F32, name="total")
-                mixed = work.tile([P, S], F32, name="mixed")
-                summed = K - 1 if last_unit else K
-                for k in range(K):
-                    cuts = [0, FIRST, S] if first_unit and k == 0 else [0, S]
+            ending = b == blocks - 1
+            groups = [[m] for m in range(M - 2)] + [[M - 2, M - 1]] if ending else [[m] for m in range(M)]
+            for group in groups:
+                paired = len(group) > 1
+
+                def look_up(m, k):
+                    product = work.tile([P, S], F32, name="product")
+                    cuts = [0, FIRST, S] if b == 0 and m == 0 and k == 0 else [0, S]
                     for low, high in zip(cuts[:-1], cuts[1:]):
                         entries = slice(k * S + low, k * S + high)
                         nc.vector.tensor_tensor(
-                            product[:, entries],
+                            product[:, low:high],
                             windows[b][:].indirect(offsets[:, entries.start // PER_COLUMN : entries.stop // PER_COLUMN]),
-                            weight[:, entries],
+                            weights[m][:, entries],
                             MULT,
                         )
-                    if k < summed:
-                        nc.tensor.matmul(total[:], identity[:], product[:, k * S : (k + 1) * S], start=(k == 0), stop=(k == summed - 1))
-                if last_unit:
-                    nc.vector.tensor_tensor(mixed[:], product[:, (K - 1) * S : K * S], total[:], ADD)
-                else:
-                    nc.scalar.copy(mixed[:], total[:])
-                nc.scalar.dma_start(out[rows, m * S : (m + 1) * S], mixed[:])
+                    return product
+
+                summed = K - 1 if paired else K
+                totals = {}
+                for m in group:
+                    total = psum.tile([P, S], F32, name="total")
+                    for k in range(summed):
+                        product = look_up(m, k)
+                        nc.tensor.matmul(total[:], identity[:], product[:], start=(k == 0), stop=(k == summed - 1))
+                    totals[m] = total
+
+                lasts = {m: look_up(m, K - 1) for m in group} if paired else {}
+                for m in group:
+                    mixed = work.tile([P, S], F32, name="mixed")
+                    if paired:
+                        nc.vector.tensor_tensor(mixed[:], lasts[m][:], totals[m][:], ADD)
+                    else:
+                        nc.scalar.copy(mixed[:], totals[m][:])
+                    nc.scalar.dma_start(out[rows, m * S : (m + 1) * S], mixed[:])

import concourse.mybir as mybir
from concourse.masks import make_identity

F32 = mybir.dt.float32
U16 = mybir.dt.uint16
MULT = mybir.AluOpType.mult
ADD = mybir.AluOpType.add

P = 128
C = 256
S = 256
K = 4
M = 4
N = K * S
PER_COLUMN = 16
PIECES = 2 * K
FIRST = 64

BYTES = C * S * 4 + M * N * 4 + P * (N // PER_COLUMN) * 2 + C * M * S * 4


def tile_paiconvmax_kernel(tc, x, perm, offs, out):
    nc = tc.nc
    blocks = C // P
    with (
        tc.tile_pool(name="held", bufs=1) as held,
        tc.tile_pool(name="work", bufs=PIECES) as work,
        tc.psum_pool(name="psum", bufs=4) as psum,
    ):
        offsets = held.tile([P, N // PER_COLUMN], U16, name="offsets")

        windows = [held.tile([P, S], F32, name=f"window{b}") for b in range(blocks)]
        weights = [held.tile([P, N], F32, name=f"weight{m}") for m in range(M)]
        nc.scalar.dma_start(windows[0][:], x[0:P, :])
        nc.sync.dma_start(weights[0][:, :FIRST], perm[0:P, :FIRST])
        nc.sync.dma_start(offsets[:], offs)
        nc.scalar.dma_start(weights[0][:, FIRST:S], perm[0:P, FIRST:S])
        asked = S
        while asked < M * N:
            m, start = divmod(asked, N)
            width = min(max(asked // (2 * S), 1) * S, N - start)
            nc.scalar.dma_start(weights[m][:, start : start + width], perm[0:P, asked : asked + width])
            asked += width
        nc.scalar.dma_start(windows[1][:], x[P : 2 * P, :])

        identity = held.tile([P, P], F32, name="identity")
        make_identity(nc, identity[:])

        for b in range(blocks):
            rows = slice(b * P, (b + 1) * P)
            ending = b == blocks - 1
            groups = [[m] for m in range(M - 2)] + [[M - 2, M - 1]] if ending else [[m] for m in range(M)]
            for group in groups:
                paired = len(group) > 1

                def look_up(m, k):
                    product = work.tile([P, S], F32, name="product")
                    cuts = [0, FIRST, S] if b == 0 and m == 0 and k == 0 else [0, S]
                    for low, high in zip(cuts[:-1], cuts[1:]):
                        entries = slice(k * S + low, k * S + high)
                        nc.vector.tensor_tensor(
                            product[:, low:high],
                            windows[b][:].indirect(offsets[:, entries.start // PER_COLUMN : entries.stop // PER_COLUMN]),
                            weights[m][:, entries],
                            MULT,
                        )
                    return product

                summed = K - 1 if paired else K
                totals = {}
                for m in group:
                    total = psum.tile([P, S], F32, name="total")
                    for k in range(summed):
                        product = look_up(m, k)
                        nc.tensor.matmul(total[:], identity[:], product[:], start=(k == 0), stop=(k == summed - 1))
                    totals[m] = total

                lasts = {m: look_up(m, K - 1) for m in group} if paired else {}
                for m in group:
                    mixed = work.tile([P, S], F32, name="mixed")
                    if paired:
                        nc.vector.tensor_tensor(mixed[:], lasts[m][:], totals[m][:], ADD)
                    else:
                        nc.scalar.copy(mixed[:], totals[m][:])
                    nc.scalar.dma_start(out[rows, m * S : (m + 1) * S], mixed[:])
